import numpy as np
import ml_dtypes


def mxq(x, axis, fmt="e4m3"):
    dtype, down = {"e4m3": (ml_dtypes.float8_e4m3fn, 7), "e5m2": (ml_dtypes.float8_e5m2, 14)}[fmt]
    v = np.moveaxis(np.asarray(x, np.float32).astype(ml_dtypes.bfloat16).astype(np.float64), axis, -1)
    blocks = v.reshape(v.shape[:-1] + (-1, 32))
    amax = np.abs(blocks).max(-1, keepdims=True)
    byte = np.maximum(np.where(amax > 0, np.frexp(amax)[1] - 1 + 127, 0) - down, 1)
    scale = np.exp2(byte - 127.0)
    codes = (blocks / scale).astype(np.float32).astype(dtype).astype(np.float64)
    return np.moveaxis((codes * scale).reshape(v.shape), -1, axis)


WIDE = False


def mx_kscale(k):
    if not WIDE:
        return np.ones(k)
    levels = np.array([10, -10, 5, -5, 0])
    if k % 512:
        return np.exp2(np.random.permutation(np.resize(levels, k // 32))).repeat(32)
    a = np.empty((k // 512, 16))
    for p in range(k // 512):
        a[p, :8] = np.random.permutation(np.resize(levels, 8))
        for g in range(8):
            far = levels[np.abs(levels - a[p, g]) >= 10]
            a[p, g + 8] = far[np.random.randint(len(far))]
    return np.exp2(a.ravel()).repeat(32)


BF16 = ml_dtypes.bfloat16


def bf(x):
    return np.asarray(x, np.float32).astype(BF16)


def f64(x):
    return np.asarray(x).astype(np.float64)


B, N, DIM, H, HKV, D, CACHE, WINDOW = 4, 2048, 512, 2, 1, 128, 1536, 1024
EPS = 1e-6
THETA = 10000.0
HALF = D // 2


def rms_norm(t, w):
    return t * (1.0 / np.sqrt(np.mean(t * t, axis=-1, keepdims=True) + EPS)) * w


def rope(t, cos, sin):
    t2 = t.reshape(*t.shape[:-1], HALF, 2)
    x0, x1 = t2[..., 0], t2[..., 1]
    c = cos[None, None, :, :]
    s = sin[None, None, :, :]
    r0 = x0 * c - x1 * s
    r1 = x0 * s + x1 * c
    return np.stack([r0, r1], axis=-1).reshape(t.shape)


def setup_inputs():
    s = mx_kscale(DIM)
    ang = np.arange(CACHE, CACHE + N)[:, None] * (1.0 / THETA ** (np.arange(0, D, 2) / D))[None, :]
    return {"x": bf(np.random.standard_normal((B, N, DIM)) * s),
            "freqs_cos": bf(np.cos(ang)), "freqs_sin": bf(np.sin(ang)),
            "Wq": bf(np.random.standard_normal((H * D, DIM)) / np.sqrt(DIM) / s[None, :]),
            "Wk": bf(np.random.standard_normal((HKV * D, DIM)) / np.sqrt(DIM) / s[None, :]),
            "Wv": bf(np.random.standard_normal((HKV * D, DIM)) / np.sqrt(DIM) / s[None, :]),
            "wq_norm": bf(2.0 + 0.2 * np.random.standard_normal(D)),
            "wk_norm": bf(1.0 + 0.1 * np.random.standard_normal(D))}


def reference(x, freqs_cos, freqs_sin, Wq, Wk, Wv, wq_norm, wk_norm):
    xq = mxq(f64(x), 2, "e4m3")
    q = (xq @ mxq(f64(Wq), 1, "e4m3").T).reshape(B, N, H, D).transpose(0, 2, 1, 3)
    k = (xq @ mxq(f64(Wk), 1, "e4m3").T).reshape(B, N, HKV, D).transpose(0, 2, 1, 3)
    v = (xq @ mxq(f64(Wv), 1, "e4m3").T).reshape(B, N, HKV, D).transpose(0, 2, 1, 3)
    q = rms_norm(q, f64(wq_norm))
    k = rms_norm(k, f64(wk_norm))
    q = rope(q, f64(freqs_cos), f64(freqs_sin))
    k = rope(k, f64(freqs_cos), f64(freqs_sin))
    return q, k, v

@@ -1,0 +1,308 @@
+from contextlib import ExitStack
+
+import concourse.mybir as mybir
+from concourse.masks import make_identity
+
+F32 = mybir.dt.float32
+BF16 = mybir.dt.bfloat16
+U32 = mybir.dt.uint32
+U8 = mybir.dt.uint8
+FP8X4 = mybir.dt.float8_e4m3fn_x4
+ALU = mybir.AluOpType
+ACT = mybir.ActivationFunctionType
+
+P = 128
+B, N, DIM, D = 4, 2048, 512, 128
+HALF = D // 2
+EPS = 1e-6
+N_HEADS = 4
+N_ROTATED = 3
+V_HEAD = 3
+WORDS = DIM // 2
+PACK = 4
+
+J = 8
+CHUNK = P * J
+HALVES = N // CHUNK
+POSITION_TILES = HALVES * J
+GROUP = 4
+PAIRS_PER_GROUP = GROUP // 2
+GROUPS_PER_CHUNK = J // GROUP
+N_GROUPS = B * HALVES * GROUPS_PER_CHUNK
+N_PAIRS = N_GROUPS * PAIRS_PER_GROUP
+N_TABLE_PIECES = (POSITION_TILES // GROUP) * 2 * 2
+
+FLOPS = 2 * B * N * DIM * (N_HEADS * D)
+
+
+def place_of_group(group):
+    chunk, part_of_chunk = divmod(group, GROUPS_PER_CHUNK)
+    half, b = divmod(chunk, B)
+    return b, half, part_of_chunk * GROUP
+
+
+def tile_slidingcacheattention_pa_t_kernel(
+    tc, x, freqs_cos, freqs_sin, Wq, Wk, Wv, wq_norm, wk_norm, out_0, out_1, out_2
+):
+    nc = tc.nc
+    with ExitStack() as ctx:
+        ctx.enter_context(tc.manual_schedule())
+        const = ctx.enter_context(tc.tile_pool(name="const", bufs=1))
+        x_pool = ctx.enter_context(tc.tile_pool(name="x_pool", bufs=N_GROUPS))
+        mx_pool = ctx.enter_context(tc.tile_pool(name="mx_pool", bufs=2))
+        small = ctx.enter_context(tc.tile_pool(name="small", bufs=3))
+        parts = ctx.enter_context(tc.tile_pool(name="parts", bufs=3))
+        stores = ctx.enter_context(tc.tile_pool(name="stores", bufs=4))
+        turn_psum = ctx.enter_context(tc.psum_pool(name="turn_psum", bufs=2))
+        acc_psum = ctx.enter_context(tc.psum_pool(name="acc_psum", bufs=6))
+
+        w_rows = const.tile([P, N_HEADS * DIM], BF16)
+        nc.sync.dma_start(
+            out=w_rows[:, 0 : 2 * DIM].rearrange("p (f k) -> p f k", f=2),
+            in_=Wq.rearrange("(f p) k -> p f k", p=P),
+        )
+        nc.sync.dma_start(out=w_rows[:, 2 * DIM : 3 * DIM], in_=Wk)
+        nc.sync.dma_start(out=w_rows[:, 3 * DIM : 4 * DIM], in_=Wv)
+
+        x_words = []
+        for group in range(N_GROUPS):
+            b, half, first_tile = place_of_group(group)
+            x_rows = x_pool.tile([P, GROUP * DIM], BF16, name="x_rows", tag="x_rows")
+            nc.sync.dma_start(
+                out=x_rows[:].rearrange("p (j k) -> p j k", j=GROUP),
+                in_=x[b, half * CHUNK : (half + 1) * CHUNK, :].rearrange("(p j) k -> p j k", j=J)[
+                    :, first_tile : first_tile + GROUP, :
+                ],
+            )
+            x_words.append(x_rows[:].bitcast(F32))
+
+        cos_sin = const.tile([P, 3, POSITION_TILES, HALF], BF16)
+        for plane, freqs in enumerate((freqs_cos, freqs_sin, freqs_cos)):
+            nc.scalar.dma_start(
+                out=cos_sin[:, plane, :, :].rearrange("p (c j) i -> p c (j i)", c=HALVES),
+                in_=freqs.rearrange("(c p j) i -> p c (j i)", c=HALVES, p=P),
+            )
+        gain_rows = const.tile([P, 2, D], BF16)
+        nc.scalar.dma_start(out=gain_rows[:, 0, :], in_=wq_norm.partition_broadcast(P))
+        nc.scalar.dma_start(out=gain_rows[:, 1, :], in_=wk_norm.partition_broadcast(P))
+
+        ident = const.tile([P, P], F32)
+        make_identity(nc, ident[:])
+        eps = const.tile([P, 1], F32)
+        nc.vector.memset(eps[:], EPS)
+        warm = const.tile([P, 1], F32)
+        nc.scalar.activation(out=warm[:], in_=eps[:], func=ACT.Abs_reciprocal_sqrt)
+
+        def transpose_two_tiles(words, first_word):
+            bank = turn_psum.tile([P, 2, 2, P], F32, name="bank", tag="bank")
+            for t in range(2):
+                for u in range(2):
+                    start = first_word + t * WORDS
+                    nc.tensor.transpose(
+                        out=bank[:, t, u, :],
+                        in_=words[:, start + u : start + WORDS : 2],
+                        identity=ident[:],
+                    )
+            return bank
+
+        gains = const.tile([P, 2, 2, HALF, 2], F32)
+        gain_pairs = gain_rows[:].rearrange("p k (i e) -> p k i e", e=2)
+        nc.vector.tensor_copy(
+            out=gains[:, :, 0, :, :], in_=gain_pairs[:, :, :, 0:1].to_broadcast([P, 2, HALF, 2])
+        )
+        nc.vector.tensor_scalar_mul(
+            out=gains[:, :, 1, :, 0:1], in0=gain_pairs[:, :, :, 1:2], scalar1=-1.0
+        )
+        nc.vector.tensor_copy(out=gains[:, :, 1, :, 1:2], in_=gain_pairs[:, :, :, 1:2])
+
+        table = [
+            const.tile([P, POSITION_TILES, 2, D], F32, name="table_q"),
+            const.tile([P, POSITION_TILES, 2, D], F32, name="table_k"),
+        ]
+
+        def build_table_piece(piece):
+            position_group, kind_part = divmod(piece, 4)
+            kind, part = divmod(kind_part, 2)
+            tiles = slice(position_group * GROUP, (position_group + 1) * GROUP)
+            nc.vector.tensor_tensor(
+                out=table[kind][:, tiles, part, :].rearrange("p t (i e) -> p t i e", e=2),
+                in0=cos_sin[:, part : part + 2, tiles, :].rearrange("p e t i -> p t i e"),
+                in1=gains[:, kind, part, :, :].unsqueeze(1).to_broadcast([P, GROUP, HALF, 2]),
+                op=ALU.mult,
+            )
+
+        for piece in range(4):
+            build_table_piece(piece)
+
+        w_grouped = const.tile([P, N_HEADS * D * PACK], BF16, align_bytes=64)
+        w_codes = const.tile([P, N_HEADS * D], U32, align_bytes=64)
+        w_scales = const.tile([P, N_HEADS * D], U8, align_bytes=64)
+        w_words = w_rows[:].bitcast(F32)
+        for f2 in range(N_HEADS // 2):
+            bank = transpose_two_tiles(w_words, f2 * 2 * WORDS)
+            for t in range(2):
+                f = 2 * f2 + t
+                grouped_words = w_grouped[:, f * D * PACK : (f + 1) * D * PACK].bitcast(F32)
+                if f == V_HEAD:
+                    nc.scalar.copy(
+                        out=grouped_words.rearrange("p (r u) -> p r u", u=2),
+                        in_=bank[:, t, :, :].rearrange("p u r -> p r u"),
+                    )
+                else:
+                    nc.scalar.copy(
+                        out=grouped_words.rearrange("p (a i u) -> p a i u", a=2, u=2),
+                        in_=bank[:, t, :, :].rearrange("p u (i a) -> p a i u", a=2),
+                    )
+        nc.vector.quantize_mx(out=w_codes[:].bitcast(FP8X4), scales=w_scales[:], in_=w_grouped[:])
+
+        banks, grouped_tiles, codes, accs, rstds, part_tiles, store_tiles = {}, {}, {}, {}, {}, {}, {}
+
+        def stage_transpose(g):
+            group, pair = divmod(g, PAIRS_PER_GROUP)
+            banks[g] = transpose_two_tiles(x_words[group], pair * 2 * WORDS)
+
+        def stage_regroup(g):
+            group, pair = divmod(g, PAIRS_PER_GROUP)
+            if pair == 0:
+                grouped_tiles[group] = mx_pool.tile(
+                    [P, GROUP * P * PACK], BF16, name="grouped", tag="grouped", align_bytes=64
+                )
+            columns = slice(pair * 2 * P * PACK, (pair + 1) * 2 * P * PACK)
+            nc.scalar.copy(
+                out=grouped_tiles[group][:, columns].bitcast(F32).rearrange("p (t r u) -> p t r u", t=2, u=2),
+                in_=banks[g][:].rearrange("p t u r -> p t r u"),
+            )
+
+        def stage_quantise(group):
+            x_codes = mx_pool.tile([P, GROUP * P], U32, name="x_codes", tag="x_codes", align_bytes=64)
+            x_scales = mx_pool.tile([P, GROUP * P], U8, name="x_scales", tag="x_scales", align_bytes=64)
+            nc.vector.quantize_mx(
+                out=x_codes[:].bitcast(FP8X4), scales=x_scales[:], in_=grouped_tiles[group][:]
+            )
+            codes[group] = (x_codes, x_scales)
+            for piece in range(4 * (group + 1), 4 * (group + 2)):
+                if piece < N_TABLE_PIECES:
+                    build_table_piece(piece)
+
+        def stage_matmul(g):
+            group, pair = divmod(g, PAIRS_PER_GROUP)
+            x_codes, x_scales = codes[group]
+            accs[g] = []
+            for t in range(2):
+                tokens = slice((2 * pair + t) * P, (2 * pair + t + 1) * P)
+                acc = acc_psum.tile([P, N_HEADS * D], F32, name="acc", tag="acc")
+                nc.tensor.matmul_mx(
+                    out=acc[:],
+                    lhsT=x_codes[:, tokens].bitcast(FP8X4),
+                    lhsT_scale=x_scales[:, tokens],
+                    rhs=w_codes[:].bitcast(FP8X4),
+                    rhs_scale=w_scales[:],
+                    start=True,
+                    stop=True,
+                )
+                accs[g].append(acc)
+
+        def stage_norm(g):
+            group, pair = divmod(g, PAIRS_PER_GROUP)
+            if pair == 0:
+                store_tiles[group] = stores.tile([P, N_HEADS, GROUP, D], F32, name="staged", tag="staged")
+            squares = small.tile([P, 2 * N_ROTATED, D], BF16, name="squares", tag="squares")
+            sums = small.tile([P, 2 * N_ROTATED], F32, name="sums", tag="sums")
+            rstd = small.tile([P, 2 * N_ROTATED], F32, name="rstd", tag="rstd")
+            for t in range(2):
+                for h in range(N_ROTATED):
+                    row = t * N_ROTATED + h
+                    nc.scalar.activation(
+                        out=squares[:, row, :],
+                        in_=accs[g][t][:, h * D : (h + 1) * D],
+                        func=ACT.Square,
+                        accum_out=sums[:, row : row + 1],
+                    )
+            for t in range(2):
+                nc.scalar.copy(
+                    out=store_tiles[group][:, V_HEAD, 2 * pair + t, :],
+                    in_=accs[g][t][:, V_HEAD * D : (V_HEAD + 1) * D],
+                )
+            nc.scalar.activation(
+                out=rstd[:], in_=sums[:], func=ACT.Abs_reciprocal_sqrt, scale=1.0 / D, bias=eps[:]
+            )
+            rstds[g] = rstd
+            if pair == PAIRS_PER_GROUP - 1:
+                b, half, first_tile = place_of_group(group)
+                nc.sync.dma_start(
+                    out=out_2[b, 0, half * CHUNK : (half + 1) * CHUNK, :].rearrange("(p j) d -> p j d", j=J)[
+                        :, first_tile : first_tile + GROUP, :
+                    ],
+                    in_=store_tiles[group][:, V_HEAD, :, :],
+                )
+
+        def product(g, row):
+            group, pair = divmod(g, PAIRS_PER_GROUP)
+            if pair == 0 and row == 0:
+                part_tiles[group] = parts.tile(
+                    [P, GROUP, N_ROTATED, 2, D], F32, name="even_odd", tag="even_odd"
+                )
+            t, h = divmod(row, N_ROTATED)
+            b, half, first_tile = place_of_group(group)
+            tile_in_group = 2 * pair + t
+            position_tile = half * J + first_tile + tile_in_group
+            kind = 0 if h < 2 else 1
+            nc.vector.scalar_tensor_tensor(
+                out=part_tiles[group][:, tile_in_group, h, :, :].rearrange("p a (i e) -> p (a i) e", e=2),
+                in0=accs[g][t][:, h * D : (h + 1) * D].unsqueeze(2).to_broadcast([P, D, 2]),
+                scalar=rstds[g][:, row : row + 1],
+                in1=table[kind][:, position_tile, :, :].rearrange("p a (i e) -> p (a i) e", e=2),
+                op0=ALU.mult,
+                op1=ALU.mult,
+            )
+
+        def stage_sum(group, start, count):
+            staged = store_tiles[group]
+            own = slice(start, start + count)
+            nc.gpsimd.tensor_tensor(
+                out=staged[:, 0:N_ROTATED, own, :].rearrange("p h t d -> p t h d"),
+                in0=part_tiles[group][:, own, :, 0, :],
+                in1=part_tiles[group][:, own, :, 1, :],
+                op=ALU.add,
+            )
+            b, half, first_tile = place_of_group(group)
+            tokens = slice(half * CHUNK, (half + 1) * CHUNK)
+            tiles = slice(first_tile + start, first_tile + start + count)
+            nc.sync.dma_start(
+                out=out_0[b, :, tokens, :].rearrange("h (p j) d -> p h j d", j=J)[:, :, tiles, :],
+                in_=staged[:, 0:2, own, :],
+            )
+            nc.sync.dma_start(
+                out=out_1[b, 0, tokens, :].rearrange("(p j) d -> p j d", j=J)[:, tiles, :],
+                in_=staged[:, 2, own, :],
+            )
+
+        def in_range(g):
+            return 0 <= g < N_PAIRS
+
+        def ends_group(g):
+            return in_range(g) and g % PAIRS_PER_GROUP == PAIRS_PER_GROUP - 1
+
+        last_row = 2 * N_ROTATED - 1
+        for step in range(-5, N_PAIRS + 3):
+            if in_range(step + 1):
+                stage_matmul(step + 1)
+            if in_range(step + 5):
+                stage_transpose(step + 5)
+            if in_range(step):
+                stage_norm(step)
+            if in_range(step + 4):
+                stage_regroup(step + 4)
+            if in_range(step - 1):
+                for row in range(last_row):
+                    product(step - 1, row)
+            if ends_group(step + 3):
+                stage_quantise((step + 3) // PAIRS_PER_GROUP)
+            if in_range(step - 1):
+                product(step - 1, last_row)
+            if in_range(step - 2):
+                group, pair = divmod(step - 2, PAIRS_PER_GROUP)
+                if group == N_GROUPS - 1:
+                    stage_sum(group, 2 * pair, 2)
+                elif pair == PAIRS_PER_GROUP - 1:
+                    stage_sum(group, 0, GROUP)

@@ -26,19 +26,26 @@ CHUNK = P * J
 HALVES = N // CHUNK
 POSITION_TILES = HALVES * J
 GROUP = 4
-PAIRS_PER_GROUP = GROUP // 2
+PAIR = 2
+PAIRS_PER_GROUP = GROUP // PAIR
 GROUPS_PER_CHUNK = J // GROUP
-N_GROUPS = B * HALVES * GROUPS_PER_CHUNK
+POSITION_GROUPS = POSITION_TILES // GROUP
+N_GROUPS = B * POSITION_GROUPS
 N_PAIRS = N_GROUPS * PAIRS_PER_GROUP
-N_TABLE_PIECES = (POSITION_TILES // GROUP) * 2 * 2
+PIECES = 4
 
 FLOPS = 2 * B * N * DIM * (N_HEADS * D)
 
 
+def place_of_position_group(position_group):
+    half, part = divmod(position_group, GROUPS_PER_CHUNK)
+    return half, part * GROUP
+
+
 def place_of_group(group):
-    chunk, part_of_chunk = divmod(group, GROUPS_PER_CHUNK)
-    half, b = divmod(chunk, B)
-    return b, half, part_of_chunk * GROUP
+    position_group, b = divmod(group, B)
+    half, first_tile = place_of_position_group(position_group)
+    return b, half, first_tile
 
 
 def tile_slidingcacheattention_pa_t_kernel(
@@ -49,52 +56,69 @@ def tile_slidingcacheattention_pa_t_kernel(
         ctx.enter_context(tc.manual_schedule())
         const = ctx.enter_context(tc.tile_pool(name="const", bufs=1))
         x_pool = ctx.enter_context(tc.tile_pool(name="x_pool", bufs=N_GROUPS))
-        mx_pool = ctx.enter_context(tc.tile_pool(name="mx_pool", bufs=2))
+        mx_pool = ctx.enter_context(tc.tile_pool(name="mx_pool", bufs=3))
         small = ctx.enter_context(tc.tile_pool(name="small", bufs=3))
         parts = ctx.enter_context(tc.tile_pool(name="parts", bufs=3))
         stores = ctx.enter_context(tc.tile_pool(name="stores", bufs=4))
         turn_psum = ctx.enter_context(tc.psum_pool(name="turn_psum", bufs=2))
         acc_psum = ctx.enter_context(tc.psum_pool(name="acc_psum", bufs=6))
 
+        eps = const.tile([P, 1], F32)
+        nc.vector.memset(eps[:], EPS)
+        warm = const.tile([P, 1], F32)
+        nc.scalar.activation(out=warm[:], in_=eps[:], func=ACT.Abs_reciprocal_sqrt)
+        gain_rows = const.tile([P, 2 * D], BF16)
+        nc.vector.memset(gain_rows[:], 0.0)
+        ones = const.tile([P, P], BF16)
+        nc.vector.memset(ones[:], 1.0)
+        ident = const.tile([P, P], F32)
+        make_identity(nc, ident[:])
+
         w_rows = const.tile([P, N_HEADS * DIM], BF16)
+        cos_sin = const.tile([P, 3, POSITION_TILES, HALF], BF16)
+        x_words = []
+
+        def load_cos_sin(queue, position_group):
+            half, first_tile = place_of_position_group(position_group)
+            tiles = slice(position_group * GROUP, (position_group + 1) * GROUP)
+            for plane, freqs in enumerate((freqs_cos, freqs_sin, freqs_cos)):
+                queue.dma_start(
+                    out=cos_sin[:, plane, tiles, :],
+                    in_=freqs[half * CHUNK : (half + 1) * CHUNK, :].rearrange("(p j) i -> p j i", j=J)[
+                        :, first_tile : first_tile + GROUP, :
+                    ],
+                )
+
+        def load_x(group, pieces):
+            b, half, first_tile = place_of_group(group)
+            x_rows = x_pool.tile([P, GROUP * DIM], BF16, name="x_rows", tag="x_rows")
+            tiles = GROUP // pieces
+            for piece in range(pieces):
+                start = piece * tiles
+                nc.sync.dma_start(
+                    out=x_rows[:, start * DIM : (start + tiles) * DIM].rearrange("p (j k) -> p j k", j=tiles),
+                    in_=x[b, half * CHUNK : (half + 1) * CHUNK, :].rearrange("(p j) k -> p j k", j=J)[
+                        :, first_tile + start : first_tile + start + tiles, :
+                    ],
+                )
+            x_words.append(x_rows[:].bitcast(F32))
+
+        nc.sync.dma_start(out=gain_rows[0:1, 0:D], in_=wq_norm.unsqueeze(0))
+        nc.sync.dma_start(out=gain_rows[0:1, D : 2 * D], in_=wk_norm.unsqueeze(0))
         nc.sync.dma_start(
             out=w_rows[:, 0 : 2 * DIM].rearrange("p (f k) -> p f k", f=2),
             in_=Wq.rearrange("(f p) k -> p f k", p=P),
         )
         nc.sync.dma_start(out=w_rows[:, 2 * DIM : 3 * DIM], in_=Wk)
         nc.sync.dma_start(out=w_rows[:, 3 * DIM : 4 * DIM], in_=Wv)
+        load_cos_sin(nc.scalar, 0)
+        load_x(0, PAIRS_PER_GROUP)
+        for group in range(1, N_GROUPS):
+            load_x(group, 1)
+            if group % B == 1 and group // B + 1 < POSITION_GROUPS:
+                load_cos_sin(nc.sync, group // B + 1)
 
-        x_words = []
-        for group in range(N_GROUPS):
-            b, half, first_tile = place_of_group(group)
-            x_rows = x_pool.tile([P, GROUP * DIM], BF16, name="x_rows", tag="x_rows")
-            nc.sync.dma_start(
-                out=x_rows[:].rearrange("p (j k) -> p j k", j=GROUP),
-                in_=x[b, half * CHUNK : (half + 1) * CHUNK, :].rearrange("(p j) k -> p j k", j=J)[
-                    :, first_tile : first_tile + GROUP, :
-                ],
-            )
-            x_words.append(x_rows[:].bitcast(F32))
-
-        cos_sin = const.tile([P, 3, POSITION_TILES, HALF], BF16)
-        for plane, freqs in enumerate((freqs_cos, freqs_sin, freqs_cos)):
-            nc.scalar.dma_start(
-                out=cos_sin[:, plane, :, :].rearrange("p (c j) i -> p c (j i)", c=HALVES),
-                in_=freqs.rearrange("(c p j) i -> p c (j i)", c=HALVES, p=P),
-            )
-        gain_rows = const.tile([P, 2, D], BF16)
-        nc.scalar.dma_start(out=gain_rows[:, 0, :], in_=wq_norm.partition_broadcast(P))
-        nc.scalar.dma_start(out=gain_rows[:, 1, :], in_=wk_norm.partition_broadcast(P))
-
-        ident = const.tile([P, P], F32)
-        make_identity(nc, ident[:])
-        eps = const.tile([P, 1], F32)
-        nc.vector.memset(eps[:], EPS)
-        warm = const.tile([P, 1], F32)
-        nc.scalar.activation(out=warm[:], in_=eps[:], func=ACT.Abs_reciprocal_sqrt)
-
-        def transpose_two_tiles(words, first_word):
-            bank = turn_psum.tile([P, 2, 2, P], F32, name="bank", tag="bank")
+        def transpose_two_tiles(words, first_word, bank):
             for t in range(2):
                 for u in range(2):
                     start = first_word + t * WORDS
@@ -103,10 +127,11 @@ def tile_slidingcacheattention_pa_t_kernel(
                         in_=words[:, start + u : start + WORDS : 2],
                         identity=ident[:],
                     )
-            return bank
 
+        gain_bank = acc_psum.tile([P, 2 * D], F32, name="gain_bank", tag="acc")
+        nc.tensor.matmul(out=gain_bank[:], lhsT=ones[:], rhs=gain_rows[:], start=True, stop=True)
         gains = const.tile([P, 2, 2, HALF, 2], F32)
-        gain_pairs = gain_rows[:].rearrange("p k (i e) -> p k i e", e=2)
+        gain_pairs = gain_bank[:].rearrange("p (k i e) -> p k i e", k=2, e=2)
         nc.vector.tensor_copy(
             out=gains[:, :, 0, :, :], in_=gain_pairs[:, :, :, 0:1].to_broadcast([P, 2, HALF, 2])
         )
@@ -120,9 +145,8 @@ def tile_slidingcacheattention_pa_t_kernel(
             const.tile([P, POSITION_TILES, 2, D], F32, name="table_k"),
         ]
 
-        def build_table_piece(piece):
-            position_group, kind_part = divmod(piece, 4)
-            kind, part = divmod(kind_part, 2)
+        def build_table_piece(position_group, piece):
+            kind, part = divmod(piece, 2)
             tiles = slice(position_group * GROUP, (position_group + 1) * GROUP)
             nc.vector.tensor_tensor(
                 out=table[kind][:, tiles, part, :].rearrange("p t (i e) -> p t i e", e=2),
@@ -131,27 +155,25 @@ def tile_slidingcacheattention_pa_t_kernel(
                 op=ALU.mult,
             )
 
-        for piece in range(4):
-            build_table_piece(piece)
-
         w_grouped = const.tile([P, N_HEADS * D * PACK], BF16, align_bytes=64)
         w_codes = const.tile([P, N_HEADS * D], U32, align_bytes=64)
         w_scales = const.tile([P, N_HEADS * D], U8, align_bytes=64)
         w_words = w_rows[:].bitcast(F32)
-        for f2 in range(N_HEADS // 2):
-            bank = transpose_two_tiles(w_words, f2 * 2 * WORDS)
+        for f2, copy in enumerate((nc.scalar.copy, nc.vector.tensor_copy)):
+            w_bank = acc_psum.tile([P, 2, 2, P], F32, name="w_bank", tag="acc")
+            transpose_two_tiles(w_words, f2 * 2 * WORDS, w_bank)
             for t in range(2):
                 f = 2 * f2 + t
                 grouped_words = w_grouped[:, f * D * PACK : (f + 1) * D * PACK].bitcast(F32)
                 if f == V_HEAD:
-                    nc.scalar.copy(
+                    copy(
                         out=grouped_words.rearrange("p (r u) -> p r u", u=2),
-                        in_=bank[:, t, :, :].rearrange("p u r -> p r u"),
+                        in_=w_bank[:, t, :, :].rearrange("p u r -> p r u"),
                     )
                 else:
-                    nc.scalar.copy(
+                    copy(
                         out=grouped_words.rearrange("p (a i u) -> p a i u", a=2, u=2),
-                        in_=bank[:, t, :, :].rearrange("p u (i a) -> p a i u", a=2),
+                        in_=w_bank[:, t, :, :].rearrange("p u (i a) -> p a i u", a=2),
                     )
         nc.vector.quantize_mx(out=w_codes[:].bitcast(FP8X4), scales=w_scales[:], in_=w_grouped[:])
 
@@ -159,37 +181,31 @@ def tile_slidingcacheattention_pa_t_kernel(
 
         def stage_transpose(g):
             group, pair = divmod(g, PAIRS_PER_GROUP)
-            banks[g] = transpose_two_tiles(x_words[group], pair * 2 * WORDS)
+            banks[g] = turn_psum.tile([P, 2, 2, P], F32, name="bank", tag="bank")
+            transpose_two_tiles(x_words[group], pair * PAIR * WORDS, banks[g])
 
         def stage_regroup(g):
-            group, pair = divmod(g, PAIRS_PER_GROUP)
-            if pair == 0:
-                grouped_tiles[group] = mx_pool.tile(
-                    [P, GROUP * P * PACK], BF16, name="grouped", tag="grouped", align_bytes=64
-                )
-            columns = slice(pair * 2 * P * PACK, (pair + 1) * 2 * P * PACK)
+            grouped_tiles[g] = mx_pool.tile(
+                [P, PAIR * P * PACK], BF16, name="grouped", tag="grouped", align_bytes=64
+            )
             nc.scalar.copy(
-                out=grouped_tiles[group][:, columns].bitcast(F32).rearrange("p (t r u) -> p t r u", t=2, u=2),
+                out=grouped_tiles[g][:].bitcast(F32).rearrange("p (t r u) -> p t r u", t=2, u=2),
                 in_=banks[g][:].rearrange("p t u r -> p t r u"),
             )
 
-        def stage_quantise(group):
-            x_codes = mx_pool.tile([P, GROUP * P], U32, name="x_codes", tag="x_codes", align_bytes=64)
-            x_scales = mx_pool.tile([P, GROUP * P], U8, name="x_scales", tag="x_scales", align_bytes=64)
+        def stage_quantise(g):
+            x_codes = mx_pool.tile([P, PAIR * P], U32, name="x_codes", tag="x_codes", align_bytes=64)
+            x_scales = mx_pool.tile([P, PAIR * P], U8, name="x_scales", tag="x_scales", align_bytes=64)
             nc.vector.quantize_mx(
-                out=x_codes[:].bitcast(FP8X4), scales=x_scales[:], in_=grouped_tiles[group][:]
+                out=x_codes[:].bitcast(FP8X4), scales=x_scales[:], in_=grouped_tiles[g][:]
             )
-            codes[group] = (x_codes, x_scales)
-            for piece in range(4 * (group + 1), 4 * (group + 2)):
-                if piece < N_TABLE_PIECES:
-                    build_table_piece(piece)
+            codes[g] = (x_codes, x_scales)
 
         def stage_matmul(g):
-            group, pair = divmod(g, PAIRS_PER_GROUP)
-            x_codes, x_scales = codes[group]
+            x_codes, x_scales = codes[g]
             accs[g] = []
-            for t in range(2):
-                tokens = slice((2 * pair + t) * P, (2 * pair + t + 1) * P)
+            for t in range(PAIR):
+                tokens = slice(t * P, (t + 1) * P)
                 acc = acc_psum.tile([P, N_HEADS * D], F32, name="acc", tag="acc")
                 nc.tensor.matmul_mx(
                     out=acc[:],
@@ -206,10 +222,10 @@ def tile_slidingcacheattention_pa_t_kernel(
             group, pair = divmod(g, PAIRS_PER_GROUP)
             if pair == 0:
                 store_tiles[group] = stores.tile([P, N_HEADS, GROUP, D], F32, name="staged", tag="staged")
-            squares = small.tile([P, 2 * N_ROTATED, D], BF16, name="squares", tag="squares")
-            sums = small.tile([P, 2 * N_ROTATED], F32, name="sums", tag="sums")
-            rstd = small.tile([P, 2 * N_ROTATED], F32, name="rstd", tag="rstd")
-            for t in range(2):
+            squares = small.tile([P, PAIR * N_ROTATED, D], BF16, name="squares", tag="squares")
+            sums = small.tile([P, PAIR * N_ROTATED], F32, name="sums", tag="sums")
+            rstd = small.tile([P, PAIR * N_ROTATED], F32, name="rstd", tag="rstd")
+            for t in range(PAIR):
                 for h in range(N_ROTATED):
                     row = t * N_ROTATED + h
                     nc.scalar.activation(
@@ -218,9 +234,9 @@ def tile_slidingcacheattention_pa_t_kernel(
                         func=ACT.Square,
                         accum_out=sums[:, row : row + 1],
                     )
-            for t in range(2):
+            for t in range(PAIR):
                 nc.scalar.copy(
-                    out=store_tiles[group][:, V_HEAD, 2 * pair + t, :],
+                    out=store_tiles[group][:, V_HEAD, PAIR * pair + t, :],
                     in_=accs[g][t][:, V_HEAD * D : (V_HEAD + 1) * D],
                 )
             nc.scalar.activation(
@@ -236,35 +252,26 @@ def tile_slidingcacheattention_pa_t_kernel(
                     in_=store_tiles[group][:, V_HEAD, :, :],
                 )
 
-        def product(g, row):
+        def stage_products(g):
             group, pair = divmod(g, PAIRS_PER_GROUP)
-            if pair == 0 and row == 0:
-                part_tiles[group] = parts.tile(
-                    [P, GROUP, N_ROTATED, 2, D], F32, name="even_odd", tag="even_odd"
-                )
-            t, h = divmod(row, N_ROTATED)
-            b, half, first_tile = place_of_group(group)
-            tile_in_group = 2 * pair + t
-            position_tile = half * J + first_tile + tile_in_group
-            kind = 0 if h < 2 else 1
-            nc.vector.scalar_tensor_tensor(
-                out=part_tiles[group][:, tile_in_group, h, :, :].rearrange("p a (i e) -> p (a i) e", e=2),
-                in0=accs[g][t][:, h * D : (h + 1) * D].unsqueeze(2).to_broadcast([P, D, 2]),
-                scalar=rstds[g][:, row : row + 1],
-                in1=table[kind][:, position_tile, :, :].rearrange("p a (i e) -> p (a i) e", e=2),
-                op0=ALU.mult,
-                op1=ALU.mult,
-            )
+            part_tiles[g] = parts.tile([P, PAIR, N_ROTATED, 2, D], F32, name="even_odd", tag="even_odd")
+            for t in range(PAIR):
+                position_tile = (group // B) * GROUP + pair * PAIR + t
+                for h in range(N_ROTATED):
+                    row = t * N_ROTATED + h
+                    kind = 0 if h < 2 else 1
+                    nc.vector.scalar_tensor_tensor(
+                        out=part_tiles[g][:, t, h, :, :].rearrange("p a (i e) -> p (a i) e", e=2),
+                        in0=accs[g][t][:, h * D : (h + 1) * D].unsqueeze(2).to_broadcast([P, D, 2]),
+                        scalar=rstds[g][:, row : row + 1],
+                        in1=table[kind][:, position_tile, :, :].rearrange("p a (i e) -> p (a i) e", e=2),
+                        op0=ALU.mult,
+                        op1=ALU.mult,
+                    )
 
-        def stage_sum(group, start, count):
+        def store_rotated(group, start, count):
             staged = store_tiles[group]
             own = slice(start, start + count)
-            nc.gpsimd.tensor_tensor(
-                out=staged[:, 0:N_ROTATED, own, :].rearrange("p h t d -> p t h d"),
-                in0=part_tiles[group][:, own, :, 0, :],
-                in1=part_tiles[group][:, own, :, 1, :],
-                op=ALU.add,
-            )
             b, half, first_tile = place_of_group(group)
             tokens = slice(half * CHUNK, (half + 1) * CHUNK)
             tiles = slice(first_tile + start, first_tile + start + count)
@@ -277,32 +284,42 @@ def tile_slidingcacheattention_pa_t_kernel(
                 in_=staged[:, 2, own, :],
             )
 
+        def stage_sum(g):
+            group, pair = divmod(g, PAIRS_PER_GROUP)
+            own = slice(pair * PAIR, (pair + 1) * PAIR)
+            nc.gpsimd.tensor_tensor(
+                out=store_tiles[group][:, 0:N_ROTATED, own, :].rearrange("p h t d -> p t h d"),
+                in0=part_tiles[g][:, :, :, 0, :],
+                in1=part_tiles[g][:, :, :, 1, :],
+                op=ALU.add,
+            )
+            if group == N_GROUPS - 1:
+                store_rotated(group, pair * PAIR, PAIR)
+            elif pair == PAIRS_PER_GROUP - 1:
+                store_rotated(group, 0, GROUP)
+
         def in_range(g):
             return 0 <= g < N_PAIRS
 
-        def ends_group(g):
-            return in_range(g) and g % PAIRS_PER_GROUP == PAIRS_PER_GROUP - 1
-
-        last_row = 2 * N_ROTATED - 1
-        for step in range(-5, N_PAIRS + 3):
+        for step in range(-4, N_PAIRS + 1):
             if in_range(step + 1):
                 stage_matmul(step + 1)
-            if in_range(step + 5):
-                stage_transpose(step + 5)
+            if in_range(step + 4):
+                stage_transpose(step + 4)
             if in_range(step):
                 stage_norm(step)
-            if in_range(step + 4):
-                stage_regroup(step + 4)
+            if in_range(step + 3):
+                stage_regroup(step + 3)
             if in_range(step - 1):
-                for row in range(last_row):
-                    product(step - 1, row)
-            if ends_group(step + 3):
-                stage_quantise((step + 3) // PAIRS_PER_GROUP)
+                stage_products(step - 1)
+            if in_range(step + 2):
+                stage_quantise(step + 2)
+            if step == -2:
+                for piece in range(PIECES):
+                    build_table_piece(0, piece)
+            elif in_range(step - 1):
+                position_group, turn = divmod(step - 1, B * PAIRS_PER_GROUP)
+                if turn % 2 == 0 and position_group + 1 < POSITION_GROUPS:
+                    build_table_piece(position_group + 1, turn // 2)
             if in_range(step - 1):
-                product(step - 1, last_row)
-            if in_range(step - 2):
-                group, pair = divmod(step - 2, PAIRS_PER_GROUP)
-                if group == N_GROUPS - 1:
-                    stage_sum(group, 2 * pair, 2)
-                elif pair == PAIRS_PER_GROUP - 1:
-                    stage_sum(group, 0, GROUP)
+                stage_sum(step - 1)

@@ -78,15 +78,11 @@ def tile_slidingcacheattention_pa_t_kernel(
         cos_sin = const.tile([P, 3, POSITION_TILES, HALF], BF16)
         x_words = []
 
-        def load_cos_sin(queue, position_group):
-            half, first_tile = place_of_position_group(position_group)
-            tiles = slice(position_group * GROUP, (position_group + 1) * GROUP)
+        def load_cos_sin(queue, half):
             for plane, freqs in enumerate((freqs_cos, freqs_sin, freqs_cos)):
                 queue.dma_start(
-                    out=cos_sin[:, plane, tiles, :],
-                    in_=freqs[half * CHUNK : (half + 1) * CHUNK, :].rearrange("(p j) i -> p j i", j=J)[
-                        :, first_tile : first_tile + GROUP, :
-                    ],
+                    out=cos_sin[:, plane, half * J : (half + 1) * J, :],
+                    in_=freqs[half * CHUNK : (half + 1) * CHUNK, :].rearrange("(p j) i -> p j i", j=J),
                 )
 
         def load_x(group, pieces):
@@ -115,8 +111,8 @@ def tile_slidingcacheattention_pa_t_kernel(
         load_x(0, PAIRS_PER_GROUP)
         for group in range(1, N_GROUPS):
             load_x(group, 1)
-            if group % B == 1 and group // B + 1 < POSITION_GROUPS:
-                load_cos_sin(nc.sync, group // B + 1)
+            if group == B:
+                load_cos_sin(nc.sync, 1)
 
         def transpose_two_tiles(words, first_word, bank):
             for t in range(2):
@@ -145,15 +141,20 @@ def tile_slidingcacheattention_pa_t_kernel(
             const.tile([P, POSITION_TILES, 2, D], F32, name="table_k"),
         ]
 
-        def build_table_piece(position_group, piece):
+        def build_table_piece(engine, position_group, piece):
             kind, part = divmod(piece, 2)
             tiles = slice(position_group * GROUP, (position_group + 1) * GROUP)
-            nc.vector.tensor_tensor(
+            engine.tensor_tensor(
                 out=table[kind][:, tiles, part, :].rearrange("p t (i e) -> p t i e", e=2),
                 in0=cos_sin[:, part : part + 2, tiles, :].rearrange("p e t i -> p t i e"),
                 in1=gains[:, kind, part, :, :].unsqueeze(1).to_broadcast([P, GROUP, HALF, 2]),
                 op=ALU.mult,
             )
+
+        for piece in range(PIECES):
+            build_table_piece(nc.gpsimd, 1, piece)
+        for piece in range(PIECES // 2):
+            build_table_piece(nc.vector, 0, piece)
 
         w_grouped = const.tile([P, N_HEADS * D * PACK], BF16, align_bytes=64)
         w_codes = const.tile([P, N_HEADS * D], U32, align_bytes=64)
@@ -286,13 +287,21 @@ def tile_slidingcacheattention_pa_t_kernel(
 
         def stage_sum(g):
             group, pair = divmod(g, PAIRS_PER_GROUP)
-            own = slice(pair * PAIR, (pair + 1) * PAIR)
-            nc.gpsimd.tensor_tensor(
-                out=store_tiles[group][:, 0:N_ROTATED, own, :].rearrange("p h t d -> p t h d"),
-                in0=part_tiles[g][:, :, :, 0, :],
-                in1=part_tiles[g][:, :, :, 1, :],
-                op=ALU.add,
-            )
+
+            def add_parts(engine, start, count):
+                own = slice(pair * PAIR + start, pair * PAIR + start + count)
+                engine.tensor_tensor(
+                    out=store_tiles[group][:, 0:N_ROTATED, own, :].rearrange("p h t d -> p t h d"),
+                    in0=part_tiles[g][:, start : start + count, :, 0, :],
+                    in1=part_tiles[g][:, start : start + count, :, 1, :],
+                    op=ALU.add,
+                )
+
+            if g == N_PAIRS - 1:
+                add_parts(nc.gpsimd, 0, 1)
+                add_parts(nc.vector, 1, 1)
+            else:
+                add_parts(nc.gpsimd, 0, PAIR)
             if group == N_GROUPS - 1:
                 store_rotated(group, pair * PAIR, PAIR)
             elif pair == PAIRS_PER_GROUP - 1:
@@ -315,11 +324,11 @@ def tile_slidingcacheattention_pa_t_kernel(
             if in_range(step + 2):
                 stage_quantise(step + 2)
             if step == -2:
-                for piece in range(PIECES):
-                    build_table_piece(0, piece)
+                for piece in range(PIECES // 2, PIECES):
+                    build_table_piece(nc.vector, 0, piece)
             elif in_range(step - 1):
                 position_group, turn = divmod(step - 1, B * PAIRS_PER_GROUP)
-                if turn % 2 == 0 and position_group + 1 < POSITION_GROUPS:
-                    build_table_piece(position_group + 1, turn // 2)
+                if turn % 2 == 0 and position_group in (1, 2):
+                    build_table_piece(nc.vector, position_group + 1, turn // 2)
             if in_range(step - 1):
                 stage_sum(step - 1)

@@ -32,6 +32,8 @@ GROUPS_PER_CHUNK = J // GROUP
 POSITION_GROUPS = POSITION_TILES // GROUP
 N_GROUPS = B * POSITION_GROUPS
 N_PAIRS = N_GROUPS * PAIRS_PER_GROUP
+TURN_STEPS = (-1, 4, 6)
+EARLY_PIECES = 3
 PIECES = 4
 
 FLOPS = 2 * B * N * DIM * (N_HEADS * D)
@@ -73,16 +75,29 @@ def tile_slidingcacheattention_pa_t_kernel(
         nc.vector.memset(ones[:], 1.0)
         ident = const.tile([P, P], F32)
         make_identity(nc, ident[:])
+        ident_bf16 = const.tile([P, P], BF16)
+        nc.gpsimd.tensor_copy(out=ident_bf16[:], in_=ident[:])
 
         w_rows = const.tile([P, N_HEADS * DIM], BF16)
-        cos_sin = const.tile([P, 3, POSITION_TILES, HALF], BF16)
+        cos_sin = const.tile([P, 3, GROUP, HALF], BF16)
+        cos_sin_rows = const.tile([P, POSITION_TILES - GROUP, 2, HALF], BF16)
         x_words = []
 
-        def load_cos_sin(queue, half):
+        def load_first_cos_sin(queue):
             for plane, freqs in enumerate((freqs_cos, freqs_sin, freqs_cos)):
                 queue.dma_start(
-                    out=cos_sin[:, plane, half * J : (half + 1) * J, :],
-                    in_=freqs[half * CHUNK : (half + 1) * CHUNK, :].rearrange("(p j) i -> p j i", j=J),
+                    out=cos_sin[:, plane, :, :],
+                    in_=freqs[0:CHUNK, :].rearrange("(p j) i -> p j i", j=J)[:, 0:GROUP, :],
+                )
+
+        def load_cos_sin_rows(half, first_tile, count):
+            start = half * J + first_tile - GROUP
+            for plane, freqs in enumerate((freqs_cos, freqs_sin)):
+                nc.sync.dma_start(
+                    out=cos_sin_rows[:, start : start + count, plane, :],
+                    in_=freqs[half * CHUNK : (half + 1) * CHUNK, :].rearrange("(p j) i -> p j i", j=J)[
+                        :, first_tile : first_tile + count, :
+                    ],
                 )
 
         def load_x(group, pieces):
@@ -107,12 +122,14 @@ def tile_slidingcacheattention_pa_t_kernel(
         )
         nc.sync.dma_start(out=w_rows[:, 2 * DIM : 3 * DIM], in_=Wk)
         nc.sync.dma_start(out=w_rows[:, 3 * DIM : 4 * DIM], in_=Wv)
-        load_cos_sin(nc.scalar, 0)
+        load_first_cos_sin(nc.scalar)
         load_x(0, PAIRS_PER_GROUP)
         for group in range(1, N_GROUPS):
             load_x(group, 1)
+            if group == 1:
+                load_cos_sin_rows(0, GROUP, GROUP)
             if group == B:
-                load_cos_sin(nc.sync, 1)
+                load_cos_sin_rows(1, 0, J)
 
         def transpose_two_tiles(words, first_word, bank):
             for t in range(2):
@@ -128,33 +145,69 @@ def tile_slidingcacheattention_pa_t_kernel(
         nc.tensor.matmul(out=gain_bank[:], lhsT=ones[:], rhs=gain_rows[:], start=True, stop=True)
         gains = const.tile([P, 2, 2, HALF, 2], F32)
         gain_pairs = gain_bank[:].rearrange("p (k i e) -> p k i e", k=2, e=2)
-        nc.vector.tensor_copy(
+        nc.scalar.copy(
             out=gains[:, :, 0, :, :], in_=gain_pairs[:, :, :, 0:1].to_broadcast([P, 2, HALF, 2])
         )
-        nc.vector.tensor_scalar_mul(
-            out=gains[:, :, 1, :, 0:1], in0=gain_pairs[:, :, :, 1:2], scalar1=-1.0
-        )
-        nc.vector.tensor_copy(out=gains[:, :, 1, :, 1:2], in_=gain_pairs[:, :, :, 1:2])
+        nc.scalar.mul(out=gains[:, :, 1, :, 0:1], in_=gain_pairs[:, :, :, 1:2], mul=-1.0)
+        nc.scalar.copy(out=gains[:, :, 1, :, 1:2], in_=gain_pairs[:, :, :, 1:2])
 
-        table = [
-            const.tile([P, POSITION_TILES, 2, D], F32, name="table_q"),
-            const.tile([P, POSITION_TILES, 2, D], F32, name="table_k"),
-        ]
+        table = const.tile([P, POSITION_TILES, 2, 2, D], F32)
 
-        def build_table_piece(engine, position_group, piece):
+        def build_table_piece(piece):
             kind, part = divmod(piece, 2)
-            tiles = slice(position_group * GROUP, (position_group + 1) * GROUP)
-            engine.tensor_tensor(
-                out=table[kind][:, tiles, part, :].rearrange("p t (i e) -> p t i e", e=2),
+            tiles = slice(0, GROUP)
+            nc.vector.tensor_tensor(
+                out=table[:, tiles, kind, part, :].rearrange("p t (i e) -> p t i e", e=2),
                 in0=cos_sin[:, part : part + 2, tiles, :].rearrange("p e t i -> p t i e"),
                 in1=gains[:, kind, part, :, :].unsqueeze(1).to_broadcast([P, GROUP, HALF, 2]),
                 op=ALU.mult,
             )
 
-        for piece in range(PIECES):
-            build_table_piece(nc.gpsimd, 1, piece)
-        for piece in range(PIECES // 2):
-            build_table_piece(nc.vector, 0, piece)
+        for piece in range(EARLY_PIECES):
+            build_table_piece(piece)
+
+        gain_matrix = const.tile([P, 2, 2, HALF, 2], BF16)
+        for part, e, plane in ((0, 0, 0), (0, 1, 1), (1, 0, 1), (1, 1, 0)):
+            nc.gpsimd.tensor_tensor(
+                out=gain_matrix[:, :, part, :, e],
+                in0=ident[:, plane * HALF : (plane + 1) * HALF].unsqueeze(1).to_broadcast([P, 2, HALF]),
+                in1=gains[:, :, part, :, e],
+                op=ALU.mult,
+            )
+        cos_sin_turned = const.tile([P, POSITION_TILES - GROUP, P], BF16)
+        table_banks = {}
+
+        def turn_cos_sin(first_tile):
+            turned = turn_psum.tile([P, GROUP, P], BF16, name="turned", tag="bank")
+            table_banks["turned"] = turned
+            for t in range(GROUP):
+                nc.tensor.transpose(
+                    out=turned[:, t, :],
+                    in_=cos_sin_rows[:, first_tile + t, :, :].rearrange("p e i -> p (e i)"),
+                    identity=ident_bf16[:],
+                )
+
+        def copy_turned(first_tile):
+            nc.scalar.copy(
+                out=cos_sin_turned[:, first_tile : first_tile + GROUP, :], in_=table_banks["turned"][:]
+            )
+
+        def build_table_tile(tile):
+            bank = turn_psum.tile([P, 2 * 2 * D], F32, name="table_bank", tag="bank")
+            nc.tensor.matmul(
+                out=bank[:],
+                lhsT=cos_sin_turned[:, tile, :],
+                rhs=gain_matrix[:].rearrange("p k a i e -> p (k a i e)"),
+                start=True,
+                stop=True,
+            )
+            table_banks[tile] = bank
+
+        def copy_table_tile(tile):
+            nc.scalar.copy(
+                out=table[:, GROUP + tile, :, :, :].rearrange("p k a d -> p (k a d)"),
+                in_=table_banks[tile][:],
+            )
 
         w_grouped = const.tile([P, N_HEADS * D * PACK], BF16, align_bytes=64)
         w_codes = const.tile([P, N_HEADS * D], U32, align_bytes=64)
@@ -265,7 +318,7 @@ def tile_slidingcacheattention_pa_t_kernel(
                         out=part_tiles[g][:, t, h, :, :].rearrange("p a (i e) -> p (a i) e", e=2),
                         in0=accs[g][t][:, h * D : (h + 1) * D].unsqueeze(2).to_broadcast([P, D, 2]),
                         scalar=rstds[g][:, row : row + 1],
-                        in1=table[kind][:, position_tile, :, :].rearrange("p a (i e) -> p (a i) e", e=2),
+                        in1=table[:, position_tile, kind, :, :].rearrange("p a (i e) -> p (a i) e", e=2),
                         op0=ALU.mult,
                         op1=ALU.mult,
                     )
@@ -324,11 +377,17 @@ def tile_slidingcacheattention_pa_t_kernel(
             if in_range(step + 2):
                 stage_quantise(step + 2)
             if step == -2:
-                for piece in range(PIECES // 2, PIECES):
-                    build_table_piece(nc.vector, 0, piece)
-            elif in_range(step - 1):
-                position_group, turn = divmod(step - 1, B * PAIRS_PER_GROUP)
-                if turn % 2 == 0 and position_group in (1, 2):
-                    build_table_piece(nc.vector, position_group + 1, turn // 2)
+                for piece in range(EARLY_PIECES, PIECES):
+                    build_table_piece(piece)
+            if step in TURN_STEPS:
+                turn_cos_sin(TURN_STEPS.index(step) * GROUP)
+            if step - 1 in TURN_STEPS:
+                copy_turned(TURN_STEPS.index(step - 1) * GROUP)
+            tile, late = divmod(step - 1, 2)
+            if 0 <= tile < POSITION_TILES - GROUP:
+                if late:
+                    copy_table_tile(tile)
+                else:
+                    build_table_tile(tile)
             if in_range(step - 1):
                 stage_sum(step - 1)

from contextlib import ExitStack

import concourse.mybir as mybir
from concourse.masks import make_identity

F32 = mybir.dt.float32
BF16 = mybir.dt.bfloat16
U32 = mybir.dt.uint32
U8 = mybir.dt.uint8
FP8X4 = mybir.dt.float8_e4m3fn_x4
ALU = mybir.AluOpType
ACT = mybir.ActivationFunctionType

P = 128
B, N, DIM, D = 4, 2048, 512, 128
HALF = D // 2
EPS = 1e-6
N_HEADS = 4
N_ROTATED = 3
V_HEAD = 3
WORDS = DIM // 2
PACK = 4

J = 8
CHUNK = P * J
HALVES = N // CHUNK
POSITION_TILES = HALVES * J
GROUP = 4
PAIR = 2
PAIRS_PER_GROUP = GROUP // PAIR
GROUPS_PER_CHUNK = J // GROUP
POSITION_GROUPS = POSITION_TILES // GROUP
N_GROUPS = B * POSITION_GROUPS
N_PAIRS = N_GROUPS * PAIRS_PER_GROUP
TURN_STEPS = (-1, 4, 6)
EARLY_PIECES = 3
PIECES = 4

FLOPS = 2 * B * N * DIM * (N_HEADS * D)


def place_of_position_group(position_group):
    half, part = divmod(position_group, GROUPS_PER_CHUNK)
    return half, part * GROUP


def place_of_group(group):
    position_group, b = divmod(group, B)
    half, first_tile = place_of_position_group(position_group)
    return b, half, first_tile


def tile_slidingcacheattention_pa_t_kernel(
    tc, x, freqs_cos, freqs_sin, Wq, Wk, Wv, wq_norm, wk_norm, out_0, out_1, out_2
):
    nc = tc.nc
    with ExitStack() as ctx:
        ctx.enter_context(tc.manual_schedule())
        const = ctx.enter_context(tc.tile_pool(name="const", bufs=1))
        x_pool = ctx.enter_context(tc.tile_pool(name="x_pool", bufs=N_GROUPS))
        mx_pool = ctx.enter_context(tc.tile_pool(name="mx_pool", bufs=3))
        small = ctx.enter_context(tc.tile_pool(name="small", bufs=3))
        parts = ctx.enter_context(tc.tile_pool(name="parts", bufs=3))
        stores = ctx.enter_context(tc.tile_pool(name="stores", bufs=4))
        turn_psum = ctx.enter_context(tc.psum_pool(name="turn_psum", bufs=2))
        acc_psum = ctx.enter_context(tc.psum_pool(name="acc_psum", bufs=6))

        eps = const.tile([P, 1], F32)
        nc.vector.memset(eps[:], EPS)
        warm = const.tile([P, 1], F32)
        nc.scalar.activation(out=warm[:], in_=eps[:], func=ACT.Abs_reciprocal_sqrt)
        gain_rows = const.tile([P, 2 * D], BF16)
        nc.vector.memset(gain_rows[:], 0.0)
        ones = const.tile([P, P], BF16)
        nc.vector.memset(ones[:], 1.0)
        ident = const.tile([P, P], F32)
        make_identity(nc, ident[:])
        ident_bf16 = const.tile([P, P], BF16)
        nc.gpsimd.tensor_copy(out=ident_bf16[:], in_=ident[:])

        w_rows = const.tile([P, N_HEADS * DIM], BF16)
        cos_sin = const.tile([P, 3, GROUP, HALF], BF16)
        cos_sin_rows = const.tile([P, POSITION_TILES - GROUP, 2, HALF], BF16)
        x_words = []

        def load_first_cos_sin(queue):
            for plane, freqs in enumerate((freqs_cos, freqs_sin, freqs_cos)):
                queue.dma_start(
                    out=cos_sin[:, plane, :, :],
                    in_=freqs[0:CHUNK, :].rearrange("(p j) i -> p j i", j=J)[:, 0:GROUP, :],
                )

        def load_cos_sin_rows(half, first_tile, count):
            start = half * J + first_tile - GROUP
            for plane, freqs in enumerate((freqs_cos, freqs_sin)):
                nc.sync.dma_start(
                    out=cos_sin_rows[:, start : start + count, plane, :],
                    in_=freqs[half * CHUNK : (half + 1) * CHUNK, :].rearrange("(p j) i -> p j i", j=J)[
                        :, first_tile : first_tile + count, :
                    ],
                )

        def load_x(group, pieces):
            b, half, first_tile = place_of_group(group)
            x_rows = x_pool.tile([P, GROUP * DIM], BF16, name="x_rows", tag="x_rows")
            tiles = GROUP // pieces
            for piece in range(pieces):
                start = piece * tiles
                nc.sync.dma_start(
                    out=x_rows[:, start * DIM : (start + tiles) * DIM].rearrange("p (j k) -> p j k", j=tiles),
                    in_=x[b, half * CHUNK : (half + 1) * CHUNK, :].rearrange("(p j) k -> p j k", j=J)[
                        :, first_tile + start : first_tile + start + tiles, :
                    ],
                )
            x_words.append(x_rows[:].bitcast(F32))

        nc.sync.dma_start(out=gain_rows[0:1, 0:D], in_=wq_norm.unsqueeze(0))
        nc.sync.dma_start(out=gain_rows[0:1, D : 2 * D], in_=wk_norm.unsqueeze(0))
        nc.sync.dma_start(
            out=w_rows[:, 0 : 2 * DIM].rearrange("p (f k) -> p f k", f=2),
            in_=Wq.rearrange("(f p) k -> p f k", p=P),
        )
        nc.sync.dma_start(out=w_rows[:, 2 * DIM : 3 * DIM], in_=Wk)
        nc.sync.dma_start(out=w_rows[:, 3 * DIM : 4 * DIM], in_=Wv)
        load_first_cos_sin(nc.scalar)
        load_x(0, PAIRS_PER_GROUP)
        for group in range(1, N_GROUPS):
            load_x(group, 1)
            if group == 1:
                load_cos_sin_rows(0, GROUP, GROUP)
            if group == B:
                load_cos_sin_rows(1, 0, J)

        def transpose_two_tiles(words, first_word, bank):
            for t in range(2):
                for u in range(2):
                    start = first_word + t * WORDS
                    nc.tensor.transpose(
                        out=bank[:, t, u, :],
                        in_=words[:, start + u : start + WORDS : 2],
                        identity=ident[:],
                    )

        gain_bank = acc_psum.tile([P, 2 * D], F32, name="gain_bank", tag="acc")
        nc.tensor.matmul(out=gain_bank[:], lhsT=ones[:], rhs=gain_rows[:], start=True, stop=True)
        gains = const.tile([P, 2, 2, HALF, 2], F32)
        gain_pairs = gain_bank[:].rearrange("p (k i e) -> p k i e", k=2, e=2)
        nc.scalar.copy(
            out=gains[:, :, 0, :, :], in_=gain_pairs[:, :, :, 0:1].to_broadcast([P, 2, HALF, 2])
        )
        nc.scalar.mul(out=gains[:, :, 1, :, 0:1], in_=gain_pairs[:, :, :, 1:2], mul=-1.0)
        nc.scalar.copy(out=gains[:, :, 1, :, 1:2], in_=gain_pairs[:, :, :, 1:2])

        table = const.tile([P, POSITION_TILES, 2, 2, D], F32)

        def build_table_piece(piece):
            kind, part = divmod(piece, 2)
            tiles = slice(0, GROUP)
            nc.vector.tensor_tensor(
                out=table[:, tiles, kind, part, :].rearrange("p t (i e) -> p t i e", e=2),
                in0=cos_sin[:, part : part + 2, tiles, :].rearrange("p e t i -> p t i e"),
                in1=gains[:, kind, part, :, :].unsqueeze(1).to_broadcast([P, GROUP, HALF, 2]),
                op=ALU.mult,
            )

        for piece in range(EARLY_PIECES):
            build_table_piece(piece)

        gain_matrix = const.tile([P, 2, 2, HALF, 2], BF16)
        for part, e, plane in ((0, 0, 0), (0, 1, 1), (1, 0, 1), (1, 1, 0)):
            nc.gpsimd.tensor_tensor(
                out=gain_matrix[:, :, part, :, e],
                in0=ident[:, plane * HALF : (plane + 1) * HALF].unsqueeze(1).to_broadcast([P, 2, HALF]),
                in1=gains[:, :, part, :, e],
                op=ALU.mult,
            )
        cos_sin_turned = const.tile([P, POSITION_TILES - GROUP, P], BF16)
        table_banks = {}

        def turn_cos_sin(first_tile):
            turned = turn_psum.tile([P, GROUP, P], BF16, name="turned", tag="bank")
            table_banks["turned"] = turned
            for t in range(GROUP):
                nc.tensor.transpose(
                    out=turned[:, t, :],
                    in_=cos_sin_rows[:, first_tile + t, :, :].rearrange("p e i -> p (e i)"),
                    identity=ident_bf16[:],
                )

        def copy_turned(first_tile):
            nc.scalar.copy(
                out=cos_sin_turned[:, first_tile : first_tile + GROUP, :], in_=table_banks["turned"][:]
            )

        def build_table_tile(tile):
            bank = turn_psum.tile([P, 2 * 2 * D], F32, name="table_bank", tag="bank")
            nc.tensor.matmul(
                out=bank[:],
                lhsT=cos_sin_turned[:, tile, :],
                rhs=gain_matrix[:].rearrange("p k a i e -> p (k a i e)"),
                start=True,
                stop=True,
            )
            table_banks[tile] = bank

        def copy_table_tile(tile):
            nc.scalar.copy(
                out=table[:, GROUP + tile, :, :, :].rearrange("p k a d -> p (k a d)"),
                in_=table_banks[tile][:],
            )

        w_grouped = const.tile([P, N_HEADS * D * PACK], BF16, align_bytes=64)
        w_codes = const.tile([P, N_HEADS * D], U32, align_bytes=64)
        w_scales = const.tile([P, N_HEADS * D], U8, align_bytes=64)
        w_words = w_rows[:].bitcast(F32)
        for f2, copy in enumerate((nc.scalar.copy, nc.vector.tensor_copy)):
            w_bank = acc_psum.tile([P, 2, 2, P], F32, name="w_bank", tag="acc")
            transpose_two_tiles(w_words, f2 * 2 * WORDS, w_bank)
            for t in range(2):
                f = 2 * f2 + t
                grouped_words = w_grouped[:, f * D * PACK : (f + 1) * D * PACK].bitcast(F32)
                if f == V_HEAD:
                    copy(
                        out=grouped_words.rearrange("p (r u) -> p r u", u=2),
                        in_=w_bank[:, t, :, :].rearrange("p u r -> p r u"),
                    )
                else:
                    copy(
                        out=grouped_words.rearrange("p (a i u) -> p a i u", a=2, u=2),
                        in_=w_bank[:, t, :, :].rearrange("p u (i a) -> p a i u", a=2),
                    )
        nc.vector.quantize_mx(out=w_codes[:].bitcast(FP8X4), scales=w_scales[:], in_=w_grouped[:])

        banks, grouped_tiles, codes, accs, rstds, part_tiles, store_tiles = {}, {}, {}, {}, {}, {}, {}

        def stage_transpose(g):
            group, pair = divmod(g, PAIRS_PER_GROUP)
            banks[g] = turn_psum.tile([P, 2, 2, P], F32, name="bank", tag="bank")
            transpose_two_tiles(x_words[group], pair * PAIR * WORDS, banks[g])

        def stage_regroup(g):
            grouped_tiles[g] = mx_pool.tile(
                [P, PAIR * P * PACK], BF16, name="grouped", tag="grouped", align_bytes=64
            )
            nc.scalar.copy(
                out=grouped_tiles[g][:].bitcast(F32).rearrange("p (t r u) -> p t r u", t=2, u=2),
                in_=banks[g][:].rearrange("p t u r -> p t r u"),
            )

        def stage_quantise(g):
            x_codes = mx_pool.tile([P, PAIR * P], U32, name="x_codes", tag="x_codes", align_bytes=64)
            x_scales = mx_pool.tile([P, PAIR * P], U8, name="x_scales", tag="x_scales", align_bytes=64)
            nc.vector.quantize_mx(
                out=x_codes[:].bitcast(FP8X4), scales=x_scales[:], in_=grouped_tiles[g][:]
            )
            codes[g] = (x_codes, x_scales)

        def stage_matmul(g):
            x_codes, x_scales = codes[g]
            accs[g] = []
            for t in range(PAIR):
                tokens = slice(t * P, (t + 1) * P)
                acc = acc_psum.tile([P, N_HEADS * D], F32, name="acc", tag="acc")
                nc.tensor.matmul_mx(
                    out=acc[:],
                    lhsT=x_codes[:, tokens].bitcast(FP8X4),
                    lhsT_scale=x_scales[:, tokens],
                    rhs=w_codes[:].bitcast(FP8X4),
                    rhs_scale=w_scales[:],
                    start=True,
                    stop=True,
                )
                accs[g].append(acc)

        def stage_norm(g):
            group, pair = divmod(g, PAIRS_PER_GROUP)
            if pair == 0:
                store_tiles[group] = stores.tile([P, N_HEADS, GROUP, D], F32, name="staged", tag="staged")
            squares = small.tile([P, PAIR * N_ROTATED, D], BF16, name="squares", tag="squares")
            sums = small.tile([P, PAIR * N_ROTATED], F32, name="sums", tag="sums")
            rstd = small.tile([P, PAIR * N_ROTATED], F32, name="rstd", tag="rstd")
            for t in range(PAIR):
                for h in range(N_ROTATED):
                    row = t * N_ROTATED + h
                    nc.scalar.activation(
                        out=squares[:, row, :],
                        in_=accs[g][t][:, h * D : (h + 1) * D],
                        func=ACT.Square,
                        accum_out=sums[:, row : row + 1],
                    )
            for t in range(PAIR):
                nc.scalar.copy(
                    out=store_tiles[group][:, V_HEAD, PAIR * pair + t, :],
                    in_=accs[g][t][:, V_HEAD * D : (V_HEAD + 1) * D],
                )
            nc.scalar.activation(
                out=rstd[:], in_=sums[:], func=ACT.Abs_reciprocal_sqrt, scale=1.0 / D, bias=eps[:]
            )
            rstds[g] = rstd
            if pair == PAIRS_PER_GROUP - 1:
                b, half, first_tile = place_of_group(group)
                nc.sync.dma_start(
                    out=out_2[b, 0, half * CHUNK : (half + 1) * CHUNK, :].rearrange("(p j) d -> p j d", j=J)[
                        :, first_tile : first_tile + GROUP, :
                    ],
                    in_=store_tiles[group][:, V_HEAD, :, :],
                )

        def stage_products(g):
            group, pair = divmod(g, PAIRS_PER_GROUP)
            part_tiles[g] = parts.tile([P, PAIR, N_ROTATED, 2, D], F32, name="even_odd", tag="even_odd")
            for t in range(PAIR):
                position_tile = (group // B) * GROUP + pair * PAIR + t
                for h in range(N_ROTATED):
                    row = t * N_ROTATED + h
                    kind = 0 if h < 2 else 1
                    nc.vector.scalar_tensor_tensor(
                        out=part_tiles[g][:, t, h, :, :].rearrange("p a (i e) -> p (a i) e", e=2),
                        in0=accs[g][t][:, h * D : (h + 1) * D].unsqueeze(2).to_broadcast([P, D, 2]),
                        scalar=rstds[g][:, row : row + 1],
                        in1=table[:, position_tile, kind, :, :].rearrange("p a (i e) -> p (a i) e", e=2),
                        op0=ALU.mult,
                        op1=ALU.mult,
                    )

        def store_rotated(group, start, count):
            staged = store_tiles[group]
            own = slice(start, start + count)
            b, half, first_tile = place_of_group(group)
            tokens = slice(half * CHUNK, (half + 1) * CHUNK)
            tiles = slice(first_tile + start, first_tile + start + count)
            nc.sync.dma_start(
                out=out_0[b, :, tokens, :].rearrange("h (p j) d -> p h j d", j=J)[:, :, tiles, :],
                in_=staged[:, 0:2, own, :],
            )
            nc.sync.dma_start(
                out=out_1[b, 0, tokens, :].rearrange("(p j) d -> p j d", j=J)[:, tiles, :],
                in_=staged[:, 2, own, :],
            )

        def stage_sum(g):
            group, pair = divmod(g, PAIRS_PER_GROUP)

            def add_parts(engine, start, count):
                own = slice(pair * PAIR + start, pair * PAIR + start + count)
                engine.tensor_tensor(
                    out=store_tiles[group][:, 0:N_ROTATED, own, :].rearrange("p h t d -> p t h d"),
                    in0=part_tiles[g][:, start : start + count, :, 0, :],
                    in1=part_tiles[g][:, start : start + count, :, 1, :],
                    op=ALU.add,
                )

            if g == N_PAIRS - 1:
                add_parts(nc.gpsimd, 0, 1)
                add_parts(nc.vector, 1, 1)
            else:
                add_parts(nc.gpsimd, 0, PAIR)
            if group == N_GROUPS - 1:
                store_rotated(group, pair * PAIR, PAIR)
            elif pair == PAIRS_PER_GROUP - 1:
                store_rotated(group, 0, GROUP)

        def in_range(g):
            return 0 <= g < N_PAIRS

        for step in range(-4, N_PAIRS + 1):
            if in_range(step + 1):
                stage_matmul(step + 1)
            if in_range(step + 4):
                stage_transpose(step + 4)
            if in_range(step):
                stage_norm(step)
            if in_range(step + 3):
                stage_regroup(step + 3)
            if in_range(step - 1):
                stage_products(step - 1)
            if in_range(step + 2):
                stage_quantise(step + 2)
            if step == -2:
                for piece in range(EARLY_PIECES, PIECES):
                    build_table_piece(piece)
            if step in TURN_STEPS:
                turn_cos_sin(TURN_STEPS.index(step) * GROUP)
            if step - 1 in TURN_STEPS:
                copy_turned(TURN_STEPS.index(step - 1) * GROUP)
            tile, late = divmod(step - 1, 2)
            if 0 <= tile < POSITION_TILES - GROUP:
                if late:
                    copy_table_tile(tile)
                else:
                    build_table_tile(tile)
            if in_range(step - 1):
                stage_sum(step - 1)
